import numpy as np
import ml_dtypes


def mxq(x, axis, fmt="e4m3"):
    dtype, down = {"e4m3": (ml_dtypes.float8_e4m3fn, 7), "e5m2": (ml_dtypes.float8_e5m2, 14)}[fmt]
    v = np.moveaxis(np.asarray(x, np.float32).astype(ml_dtypes.bfloat16).astype(np.float64), axis, -1)
    blocks = v.reshape(v.shape[:-1] + (-1, 32))
    amax = np.abs(blocks).max(-1, keepdims=True)
    byte = np.maximum(np.where(amax > 0, np.frexp(amax)[1] - 1 + 127, 0) - down, 1)
    scale = np.exp2(byte - 127.0)
    codes = (blocks / scale).astype(np.float32).astype(dtype).astype(np.float64)
    return np.moveaxis((codes * scale).reshape(v.shape), -1, axis)


WIDE = False


def mx_kscale(k):
    if not WIDE:
        return np.ones(k)
    levels = np.array([10, -10, 5, -5, 0])
    if k % 512:
        return np.exp2(np.random.permutation(np.resize(levels, k // 32))).repeat(32)
    a = np.empty((k // 512, 16))
    for p in range(k // 512):
        a[p, :8] = np.random.permutation(np.resize(levels, 8))
        for g in range(8):
            far = levels[np.abs(levels - a[p, g]) >= 10]
            a[p, g + 8] = far[np.random.randint(len(far))]
    return np.exp2(a.ravel()).repeat(32)


BF16 = ml_dtypes.bfloat16


def bf(x):
    return np.asarray(x, np.float32).astype(BF16)


def f64(x):
    return np.asarray(x).astype(np.float64)


E2M1 = np.array([0.0, 0.5, 1.0, 1.5, 2.0, 3.0, 4.0, 6.0, -0.0, -0.5, -1.0, -1.5, -2.0, -3.0, -4.0, -6.0])


def pack_weight(w, fmt):
    k, n = w.shape
    w = f64(bf(w)).reshape(k // 32, 32, n)
    amax = np.abs(w).max(1)
    if fmt == "e4m3":
        byte = np.frexp(amax)[1] - 1 + 127 - 7
    else:
        mant, ex = np.frexp(amax / 6.0)
        byte = np.where(mant > 0.5, ex, ex - 1) + 127
    byte = np.clip(np.where(amax > 0, byte, 1), 1, 254)
    scaled = (w * np.exp2(127.0 - byte)[:, None, :]).reshape(k, n).astype(np.float32)
    by_word = np.ascontiguousarray(scaled.reshape(k // 512, 128, 4, n).transpose(0, 1, 3, 2))
    if fmt == "e4m3":
        words = by_word.astype(ml_dtypes.float8_e4m3fn).view(np.uint8)
    else:
        c = by_word.astype(ml_dtypes.float4_e2m1fn).view(np.uint8) & 0xF
        words = c[..., 0::2] | (c[..., 1::2] << 4)
    return np.ascontiguousarray(words), np.ascontiguousarray(byte.astype(np.uint8).reshape(k // 512, 16, n))


def unpack_weight(words, scales, fmt):
    g, p, n, _ = words.shape
    if fmt == "e4m3":
        vals = np.ascontiguousarray(words).view(ml_dtypes.float8_e4m3fn).astype(np.float64)
    else:
        nib = np.empty((g, p, n, 4), np.uint8)
        nib[..., 0::2] = words & 0xF
        nib[..., 1::2] = words >> 4
        vals = E2M1[nib]
    vals = vals * np.repeat(np.exp2(scales.astype(np.float64) - 127.0), 8, axis=1)[..., None]
    return vals.transpose(0, 1, 3, 2).reshape(g * 512, n)


B, S, D, H, DH, DR, DKV, DQ = 2, 4096, 512, 2, 128, 64, 512, 1024
HALF = DR // 2


def rope(t, cos, sin):
    t1, t2 = t[..., 0::2], t[..., 1::2]
    c = cos[None, :, None, :]
    s = sin[None, :, None, :]
    return np.stack([t1 * c - t2 * s, t1 * s + t2 * c], axis=-1).reshape(t.shape)


def draw0():
    s, t = mx_kscale(D), mx_kscale(DKV)
    ang = np.random.uniform(0.0, 2.0 * np.pi, (S, HALF))
    x = bf(np.random.standard_normal((B, S, D)) * s)
    kv_down_words, kv_down_scales = pack_weight(np.random.standard_normal((D, DKV)) / np.sqrt(D) / s[:, None] * t, "e4m3")
    k_up_words, k_up_scales = pack_weight(np.random.standard_normal((DKV, H * DH)) / np.sqrt(DKV) / t[:, None], "e4m3")
    v_up_words, v_up_scales = pack_weight(np.random.standard_normal((DKV, H * DH)) / np.sqrt(DKV) / t[:, None], "e4m3")
    k_rope_words, k_rope_scales = pack_weight(np.random.standard_normal((D, H * DR)) / np.sqrt(D) / s[:, None], "e4m3")
    return {"x": x,
            "W_kv_down_words": kv_down_words, "W_kv_down_scales": kv_down_scales,
            "W_k_up_words": k_up_words, "W_k_up_scales": k_up_scales,
            "W_v_up_words": v_up_words, "W_v_up_scales": v_up_scales,
            "W_k_rope_words": k_rope_words, "W_k_rope_scales": k_rope_scales,
            "rope_cos": bf(np.cos(ang)), "rope_sin": bf(np.sin(ang))}


def core(x, W_kv_down_words, W_kv_down_scales, W_k_up_words, W_k_up_scales, W_v_up_words, W_v_up_scales, W_k_rope_words, W_k_rope_scales, rope_cos, rope_sin):
    xq = mxq(f64(x), 2, "e4m3")
    down_kv = xq @ unpack_weight(W_kv_down_words, W_kv_down_scales, "e4m3")
    dkv = mxq(down_kv, 2, "e4m3")
    k_c = (dkv @ unpack_weight(W_k_up_words, W_k_up_scales, "e4m3")).reshape(B, S, H, DH)
    v = (dkv @ unpack_weight(W_v_up_words, W_v_up_scales, "e4m3")).reshape(B, S, H, DH)
    k_r = (xq @ unpack_weight(W_k_rope_words, W_k_rope_scales, "e4m3")).reshape(B, S, H, DR)
    k_r = rope(k_r, f64(rope_cos), f64(rope_sin))
    k = np.concatenate([k_c, k_r], axis=-1).transpose(0, 2, 1, 3)
    return k, v.transpose(0, 2, 1, 3)


def e4m3fn_bytes(y):
    return np.clip(np.asarray(y, np.float64), -448.0, 448.0).astype(np.float32).astype(ml_dtypes.float8_e4m3fn).view(np.uint8)


def e4m3fn_values(b):
    return np.asarray(b, np.uint8).view(ml_dtypes.float8_e4m3fn).astype(np.float64)


def setup_inputs():
    d = draw0()
    x0 = np.asarray(d['x']).astype(np.float64)
    s = (np.max(np.abs(x0), axis=(0, 1), keepdims=True) / 448.0).astype(np.float32)
    out = {}
    for k, v in d.items():
        if k == 'x':
            out['x_bytes'] = e4m3fn_bytes(x0 / s.astype(np.float64))
            out['x_scale'] = s
        else:
            out[k] = v
    return out


def reference(x_bytes, x_scale, W_kv_down_words, W_kv_down_scales, W_k_up_words, W_k_up_scales, W_v_up_words, W_v_up_scales, W_k_rope_words, W_k_rope_scales, rope_cos, rope_sin):
    return core(e4m3fn_values(x_bytes) * x_scale.astype(np.float64), W_kv_down_words, W_kv_down_scales, W_k_up_words, W_k_up_scales, W_v_up_words, W_v_up_scales, W_k_rope_words, W_k_rope_scales, rope_cos, rope_sin)

@@ -1,0 +1,347 @@
+from contextlib import ExitStack
+
+import concourse.mybir as mybir
+from concourse.masks import make_identity
+
+F32 = mybir.dt.float32
+BF16 = mybir.dt.bfloat16
+I32 = mybir.dt.int32
+U32 = mybir.dt.uint32
+U8 = mybir.dt.uint8
+FP8 = mybir.dt.float8_e4m3fn
+FP8X4 = mybir.dt.float8_e4m3fn_x4
+ADD = mybir.AluOpType.add
+MULT = mybir.AluOpType.mult
+
+P = 128
+B, S, D, H, DH, DR = 2, 4096, 512, 2, 128, 64
+HALF = DR // 2
+DK = DH + DR
+ROWS = 4
+BLOCK = P * ROWS
+BLOCKS = S // BLOCK
+
+FLOPS = 2 * B * S * D * (D + 2 * H * DH + H * DR)
+
+
+def tile_multiheadlatentattention_pb_t_w8_kernel(
+    tc,
+    x_bytes,
+    x_scale,
+    down_words,
+    down_scales,
+    k_up_words,
+    k_up_scales,
+    v_up_words,
+    v_up_scales,
+    k_rope_words,
+    k_rope_scales,
+    rope_cos,
+    rope_sin,
+    keys,
+    values,
+):
+    nc = tc.nc
+
+    chunks = []
+    for b in range(B):
+        for blk in range(BLOCKS):
+            first = b == 0 and blk == 0
+            last = b == B - 1 and blk == BLOCKS - 1
+            if first or last:
+                chunks.append((b, blk, 0, 2))
+                chunks.append((b, blk, 2, 2))
+            else:
+                chunks.append((b, blk, 0, 4))
+    n = len(chunks)
+
+    with ExitStack() as ctx:
+        keep = ctx.enter_context(tc.tile_pool(name="keep", bufs=1))
+        work = ctx.enter_context(tc.tile_pool(name="work", bufs=3))
+        stage = ctx.enter_context(tc.tile_pool(name="stage", bufs=3))
+        xt_pool = ctx.enter_context(tc.psum_pool(name="xt_pool", bufs=2))
+        rope_pool = ctx.enter_context(tc.psum_pool(name="rope_pool", bufs=1))
+        acc_pool = ctx.enter_context(tc.psum_pool(name="acc_pool", bufs=5))
+        ctx.enter_context(tc.manual_schedule())
+
+        ident = keep.tile([P, P], F32)
+        make_identity(nc, ident[:])
+
+        down_plane = keep.tile([P, 512], U8, align_bytes=64)
+        up_plane = keep.tile([P, 512], U8, align_bytes=64)
+        rope_plane = keep.tile([P, P], U8, align_bytes=64)
+        nc.vector.memset(down_plane[:].bitcast(I32), 0)
+        nc.vector.memset(rope_plane[:].bitcast(I32), 0)
+        nc.vector.memset(up_plane[:].bitcast(I32), 0)
+
+        x_tiles = {}
+
+        def load_x(c):
+            b, blk, row, rows = chunks[c]
+            src = x_bytes[b, blk * BLOCK : (blk + 1) * BLOCK, :].rearrange("(p j) d -> p j d", j=ROWS)
+            x_codes = keep.tile([P, rows, D], U8, name="x_codes_%d" % c)
+            nc.sync.dma_start(out=x_codes[:], in_=src[:, row : row + rows, :])
+            x_tiles[c] = x_codes
+
+        def load_words(dst, words):
+            nc.sync.dma_start(out=dst, in_=words[0].rearrange("p n t -> p (n t)").bitcast(I32))
+
+        def load_scales(plane, cols, scales):
+            for r in range(4):
+                nc.sync.dma_start(
+                    out=plane[r:P:32, cols].bitcast(I32), in_=scales[0, r:16:4, :].bitcast(I32)
+                )
+
+        load_x(0)
+        xs = keep.tile([P, 4], F32)
+        nc.sync.dma_start(out=xs[:], in_=x_scale.rearrange("a b (p t) -> p (a b t)", t=4))
+        load_x(1)
+        down_raw = keep.tile([P, 512], I32)
+        load_words(down_raw[:], down_words)
+        load_scales(down_plane, slice(0, 512), down_scales)
+        load_x(2)
+        rope_raw = keep.tile([P, P], I32)
+        load_words(rope_raw[:], k_rope_words)
+        load_scales(rope_plane, slice(0, P), k_rope_scales)
+        cos = keep.tile([P, BLOCKS, ROWS, HALF], BF16)
+        sin_raw = keep.tile([P, BLOCKS, ROWS, HALF], BF16)
+        nc.scalar.dma_start(
+            out=cos[:].rearrange("p c j i -> p c (j i)"),
+            in_=rope_cos.rearrange("(c p j) i -> p c (j i)", p=P, j=ROWS),
+        )
+        nc.scalar.dma_start(
+            out=sin_raw[:].rearrange("p c j i -> p c (j i)"),
+            in_=rope_sin.rearrange("(c p j) i -> p c (j i)", p=P, j=ROWS),
+        )
+        up_codes = keep.tile([P, 512], I32, align_bytes=64)
+        load_words(up_codes[:, 0:256], k_up_words)
+        load_words(up_codes[:, 256:512], v_up_words)
+        load_scales(up_plane, slice(0, 256), k_up_scales)
+        load_scales(up_plane, slice(256, 512), v_up_scales)
+        for c in range(3, n):
+            load_x(c)
+
+        down_codes = keep.tile([P, 512], I32, align_bytes=64)
+        down_sc = keep.tile([P, 512], U8, align_bytes=64)
+        rope_codes = keep.tile([P, P], I32, align_bytes=64)
+        rope_sc = keep.tile([P, P], U8, align_bytes=64)
+        sin = keep.tile([P, BLOCKS * ROWS, 2, HALF], BF16)
+
+        def order_down():
+            for dst, src in ((down_codes, down_raw), (down_sc, down_plane)):
+                nc.vector.tensor_copy(
+                    out=dst[:].rearrange("p (t m) -> p m t", t=4),
+                    in_=src[:].rearrange("p (m t) -> p m t", t=4),
+                )
+
+        def order_rope():
+            for dst, src in ((rope_codes, rope_raw), (rope_sc, rope_plane)):
+                nc.vector.tensor_copy(
+                    out=dst[:].rearrange("p (h e i) -> p h i e", h=H, e=2),
+                    in_=src[:].rearrange("p (h i e) -> p h i e", h=H, e=2),
+                )
+            raw = sin_raw[:].rearrange("p c j i -> p (c j) i")
+            nc.vector.tensor_scalar(out=sin[:, :, 0, :], in0=raw, scalar1=-1.0, scalar2=None, op0=MULT)
+            nc.vector.tensor_copy(out=sin[:, :, 1, :], in_=raw)
+
+        xb_t, xt_t, gx_t, xq_t, gd_t, dq_t, rp_t, ra_t, kt_t, vt_t = {}, {}, {}, {}, {}, {}, {}, {}, {}, {}
+
+        def widen(c):
+            rows = chunks[c][3]
+            xb = work.tile([P, rows, D], BF16, align_bytes=64)
+            xb_t[c] = xb
+            src = x_tiles[c]
+            if c == 0:
+                nc.scalar.copy(out=xb[:, 0, :], in_=src[:, 0, :].bitcast(FP8))
+                nc.vector.tensor_copy(out=xb[:, 1, :], in_=src[:, 1, :].bitcast(FP8))
+            elif c == 1:
+                nc.scalar.copy(out=xb[:], in_=src[:].bitcast(FP8))
+            else:
+                nc.gpsimd.tensor_copy(out=xb[:], in_=src[:].bitcast(FP8))
+
+        def transpose(c):
+            rows = chunks[c][3]
+            words = xb_t[c][:].rearrange("p j d -> p (j d)").bitcast(F32)
+            xt_t[c] = []
+            for half in range(rows // 2):
+                xt = xt_pool.tile([P, 2, 2 * P], F32)
+                xt_t[c].append(xt)
+                for jj in range(2):
+                    base = (2 * half + jj) * (D // 2)
+                    for u in range(2):
+                        nc.tensor.transpose(
+                            xt[:, u, jj * P : (jj + 1) * P], words[:, base + u : base + D // 2 : 2], ident[:]
+                        )
+
+        def scale_x(c):
+            rows = chunks[c][3]
+            gx = work.tile([P, rows * P * 4], BF16, align_bytes=64)
+            gx_t[c] = gx
+            by = xs[:].rearrange("p (u e) -> p u e", u=2).unsqueeze(1).to_broadcast([P, 2 * P, 2, 2])
+            for half in range(rows // 2):
+                nc.vector.tensor_tensor(
+                    out=gx[:, half * 1024 : (half + 1) * 1024].rearrange("p (r u e) -> p r u e", u=2, e=2),
+                    in0=xt_t[c][half][:].bitcast(BF16).rearrange("p u (r e) -> p r u e", e=2),
+                    in1=by,
+                    op=MULT,
+                )
+
+        def quant_x(c):
+            rows = chunks[c][3]
+            xc = work.tile([P, rows * P], U32, align_bytes=64)
+            xsc = work.tile([P, rows * P], U8, align_bytes=64)
+            nc.vector.quantize_mx(out=xc[:].bitcast(FP8X4), scales=xsc[:], in_=gx_t[c][:])
+            xq_t[c] = (xc, xsc)
+
+        def start_out(c):
+            rows = chunks[c][3]
+            gd = work.tile([P, rows * P, 4], BF16, align_bytes=64)
+            gd_t[c] = gd
+
+        def down(c, j):
+            xc, xsc = xq_t[c]
+            cols = slice(j * P, (j + 1) * P)
+            acc = acc_pool.tile([P, 4, P], F32)
+            for t in range(4):
+                w_cols = slice(t * P, (t + 1) * P)
+                nc.tensor.matmul_mx(
+                    out=acc[:, t, :],
+                    lhsT=down_codes[:, w_cols].bitcast(FP8X4),
+                    lhsT_scale=down_sc[:, w_cols],
+                    rhs=xc[:, cols].bitcast(FP8X4),
+                    rhs_scale=xsc[:, cols],
+                    start=True,
+                    stop=True,
+                )
+            nc.scalar.copy(out=gd_t[c][:, cols, :], in_=acc[:].rearrange("p t n -> p n t"))
+
+        def rope_mm(c):
+            xc, xsc = xq_t[c]
+            rows = chunks[c][3]
+            rp = rope_pool.tile([P, rows, P], F32)
+            rp_t[c] = rp
+            for j in range(rows):
+                cols = slice(j * P, (j + 1) * P)
+                nc.tensor.matmul_mx(
+                    out=rp[:, j, :],
+                    lhsT=xc[:, cols].bitcast(FP8X4),
+                    lhsT_scale=xsc[:, cols],
+                    rhs=rope_codes[:].bitcast(FP8X4),
+                    rhs_scale=rope_sc[:],
+                    start=True,
+                    stop=True,
+                )
+
+        def rope_mul(c):
+            blk, row, rows = chunks[c][1:]
+            rp = rp_t[c]
+            ra = work.tile([P, rows, H, 2, HALF], F32)
+            rb = work.tile([P, rows, H, 2, HALF], F32)
+            ra_t[c] = (ra, rb)
+            by_cos = cos[:, blk, row : row + rows, :].unsqueeze(2).to_broadcast([P, rows, 2 * H, HALF])
+            nc.vector.tensor_tensor(
+                out=ra[:].rearrange("p j h e i -> p j (h e) i"),
+                in0=rp[:].rearrange("p j (g i) -> p j g i", i=HALF),
+                in1=by_cos,
+                op=MULT,
+            )
+            r0 = blk * ROWS + row
+            by_sin = sin[:, r0 : r0 + rows, :, :].unsqueeze(2).to_broadcast([P, rows, H, 2, HALF])
+            nc.vector.tensor_tensor(
+                out=rb[:],
+                in0=rp[:].rearrange("p j (h e i) -> p j h e i", h=H, e=2)[:, :, :, ::-1, :],
+                in1=by_sin,
+                op=MULT,
+            )
+
+        def rope_add(c):
+            rows = chunks[c][3]
+            ra, rb = ra_t[c]
+            kt = stage.tile([P, H, rows, DK], F32)
+            kt_t[c] = kt
+            nc.gpsimd.tensor_tensor(
+                out=kt[:, :, :, DH:DK].rearrange("p h j (i e) -> p j h i e", e=2),
+                in0=ra[:].rearrange("p j h e i -> p j h i e"),
+                in1=rb[:].rearrange("p j h e i -> p j h i e"),
+                op=ADD,
+            )
+
+        def quant_d(c):
+            rows = chunks[c][3]
+            dc = work.tile([P, rows * P], U32, align_bytes=64)
+            dsc = work.tile([P, rows * P], U8, align_bytes=64)
+            nc.vector.quantize_mx(
+                out=dc[:].bitcast(FP8X4), scales=dsc[:], in_=gd_t[c][:].rearrange("p n t -> p (n t)")
+            )
+            dq_t[c] = (dc, dsc)
+
+        def up(c, which, half):
+            dc, dsc = dq_t[c]
+            acc = acc_pool.tile([P, 2, 2 * P], F32)
+            w_cols = slice(which * 256, (which + 1) * 256)
+            for jj in range(2):
+                j = 2 * half + jj
+                cols = slice(j * P, (j + 1) * P)
+                nc.tensor.matmul_mx(
+                    out=acc[:, jj, :],
+                    lhsT=dc[:, cols].bitcast(FP8X4),
+                    lhsT_scale=dsc[:, cols],
+                    rhs=up_codes[:, w_cols].bitcast(FP8X4),
+                    rhs_scale=up_plane[:, w_cols],
+                    start=True,
+                    stop=True,
+                )
+            dst = vt_t[c][:] if which else kt_t[c][:, :, :, 0:DH]
+            nc.scalar.copy(
+                out=dst[:, :, 2 * half : 2 * half + 2, :].rearrange("p h j d -> p j h d"),
+                in_=acc[:].rearrange("p j (h d) -> p j h d", h=H),
+            )
+
+        def store(c):
+            b, blk, row, rows = chunks[c]
+            tok = slice(blk * BLOCK, (blk + 1) * BLOCK)
+            for tiles, dram in ((kt_t, keys), (vt_t, values)):
+                dst = dram[b, :, tok, :].rearrange("h (p j) d -> p h j d", j=ROWS)[:, :, row : row + rows, :]
+                nc.sync.dma_start(
+                    out=dst.rearrange("p h j d -> p h (j d)"), in_=tiles[c][:].rearrange("p h j d -> p h (j d)")
+                )
+
+        for i in range(-4, n + 1):
+            live = [k for k in range(-1, 5)]
+            on = {k: 0 <= i + k < n for k in live}
+            if on[4]:
+                widen(i + 4)
+            if i == -2:
+                order_down()
+            if i == -1:
+                order_rope()
+            if on[-1]:
+                quant_d(i - 1)
+                rope_add(i - 1)
+                vt = stage.tile([P, H, chunks[i - 1][3], DH], F32)
+                vt_t[i - 1] = vt
+            if on[1]:
+                quant_x(i + 1)
+            downs = []
+            ups = []
+            if on[0]:
+                start_out(i)
+                downs = [(down, i, j) for j in range(chunks[i][3])]
+            if on[-1]:
+                ups = [(up, i - 1, which, half) for half in range(chunks[i - 1][3] // 2) for which in range(2)]
+            steps = downs[:1]
+            rest = downs[1:]
+            for k in range(max(len(rest), len(ups))):
+                steps += rest[k : k + 1] + ups[k : k + 1]
+            for k, step in enumerate(steps):
+                step[0](*step[1:])
+                if k == 1 and on[0]:
+                    rope_mm(i)
+            if on[2]:
+                scale_x(i + 2)
+            if on[0]:
+                rope_mul(i)
+            if on[3]:
+                transpose(i + 3)
+            if on[-1]:
+                store(i - 1)

@@ -12,6 +12,7 @@ FP8 = mybir.dt.float8_e4m3fn
 FP8X4 = mybir.dt.float8_e4m3fn_x4
 ADD = mybir.AluOpType.add
 MULT = mybir.AluOpType.mult
+COPY = mybir.ActivationFunctionType.Copy
 
 P = 128
 B, S, D, H, DH, DR = 2, 4096, 512, 2, 128, 64
@@ -100,16 +101,17 @@ def tile_multiheadlatentattention_pb_t_w8_kernel(
         load_words(down_raw[:], down_words)
         load_scales(down_plane, slice(0, 512), down_scales)
         load_x(2)
-        rope_raw = keep.tile([P, P], I32)
+        rope_raw = keep.tile([P, P], I32, align_bytes=64)
         load_words(rope_raw[:], k_rope_words)
         load_scales(rope_plane, slice(0, P), k_rope_scales)
+        load_x(3)
         cos = keep.tile([P, BLOCKS, ROWS, HALF], BF16)
         sin_raw = keep.tile([P, BLOCKS, ROWS, HALF], BF16)
-        nc.scalar.dma_start(
+        nc.sync.dma_start(
             out=cos[:].rearrange("p c j i -> p c (j i)"),
             in_=rope_cos.rearrange("(c p j) i -> p c (j i)", p=P, j=ROWS),
         )
-        nc.scalar.dma_start(
+        nc.sync.dma_start(
             out=sin_raw[:].rearrange("p c j i -> p c (j i)"),
             in_=rope_sin.rearrange("(c p j) i -> p c (j i)", p=P, j=ROWS),
         )
@@ -118,31 +120,27 @@ def tile_multiheadlatentattention_pb_t_w8_kernel(
         load_words(up_codes[:, 256:512], v_up_words)
         load_scales(up_plane, slice(0, 256), k_up_scales)
         load_scales(up_plane, slice(256, 512), v_up_scales)
-        for c in range(3, n):
+        for c in range(4, n):
             load_x(c)
 
         down_codes = keep.tile([P, 512], I32, align_bytes=64)
         down_sc = keep.tile([P, 512], U8, align_bytes=64)
-        rope_codes = keep.tile([P, P], I32, align_bytes=64)
-        rope_sc = keep.tile([P, P], U8, align_bytes=64)
-        sin = keep.tile([P, BLOCKS * ROWS, 2, HALF], BF16)
+        sin = keep.tile([P, 2, BLOCKS * ROWS, HALF], BF16)
 
         def order_down():
-            for dst, src in ((down_codes, down_raw), (down_sc, down_plane)):
-                nc.vector.tensor_copy(
-                    out=dst[:].rearrange("p (t m) -> p m t", t=4),
-                    in_=src[:].rearrange("p (m t) -> p m t", t=4),
-                )
+            nc.vector.tensor_copy(
+                out=down_codes[:].rearrange("p (t m) -> p t m", t=4),
+                in_=down_raw[:].rearrange("p (m t) -> p t m", t=4),
+            )
+            nc.vector.tensor_copy(
+                out=down_sc[:].rearrange("p (t m) -> p m t", t=4),
+                in_=down_plane[:].rearrange("p (m t) -> p m t", t=4),
+            )
 
-        def order_rope():
-            for dst, src in ((rope_codes, rope_raw), (rope_sc, rope_plane)):
-                nc.vector.tensor_copy(
-                    out=dst[:].rearrange("p (h e i) -> p h i e", h=H, e=2),
-                    in_=src[:].rearrange("p (h i e) -> p h i e", h=H, e=2),
-                )
+        def order_sin():
             raw = sin_raw[:].rearrange("p c j i -> p (c j) i")
-            nc.vector.tensor_scalar(out=sin[:, :, 0, :], in0=raw, scalar1=-1.0, scalar2=None, op0=MULT)
-            nc.vector.tensor_copy(out=sin[:, :, 1, :], in_=raw)
+            nc.scalar.activation(out=sin[:, 0, :, :], in_=raw, func=COPY, scale=-1.0)
+            nc.scalar.copy(out=sin[:, 1, :, :], in_=raw)
 
         xb_t, xt_t, gx_t, xq_t, gd_t, dq_t, rp_t, ra_t, kt_t, vt_t = {}, {}, {}, {}, {}, {}, {}, {}, {}, {}
 
@@ -157,7 +155,8 @@ def tile_multiheadlatentattention_pb_t_w8_kernel(
             elif c == 1:
                 nc.scalar.copy(out=xb[:], in_=src[:].bitcast(FP8))
             else:
-                nc.gpsimd.tensor_copy(out=xb[:], in_=src[:].bitcast(FP8))
+                for j in range(rows):
+                    nc.gpsimd.tensor_copy(out=xb[:, j, :], in_=src[:, j, :].bitcast(FP8))
 
         def transpose(c):
             rows = chunks[c][3]
@@ -226,8 +225,8 @@ def tile_multiheadlatentattention_pb_t_w8_kernel(
                     out=rp[:, j, :],
                     lhsT=xc[:, cols].bitcast(FP8X4),
                     lhsT_scale=xsc[:, cols],
-                    rhs=rope_codes[:].bitcast(FP8X4),
-                    rhs_scale=rope_sc[:],
+                    rhs=rope_raw[:].bitcast(FP8X4),
+                    rhs_scale=rope_plane[:],
                     start=True,
                     stop=True,
                 )
@@ -235,34 +234,36 @@ def tile_multiheadlatentattention_pb_t_w8_kernel(
         def rope_mul(c):
             blk, row, rows = chunks[c][1:]
             rp = rp_t[c]
-            ra = work.tile([P, rows, H, 2, HALF], F32)
-            rb = work.tile([P, rows, H, 2, HALF], F32)
+            ra = work.tile([P, H, rows, DR], F32)
+            rb = work.tile([P, H, rows, DR], F32)
             ra_t[c] = (ra, rb)
-            by_cos = cos[:, blk, row : row + rows, :].unsqueeze(2).to_broadcast([P, rows, 2 * H, HALF])
-            nc.vector.tensor_tensor(
-                out=ra[:].rearrange("p j h e i -> p j (h e) i"),
-                in0=rp[:].rearrange("p j (g i) -> p j g i", i=HALF),
-                in1=by_cos,
-                op=MULT,
-            )
             r0 = blk * ROWS + row
-            by_sin = sin[:, r0 : r0 + rows, :, :].unsqueeze(2).to_broadcast([P, rows, H, 2, HALF])
+            by_cos = cos[:, blk, row : row + rows, :]
             nc.vector.tensor_tensor(
-                out=rb[:],
-                in0=rp[:].rearrange("p j (h e i) -> p j h e i", h=H, e=2)[:, :, :, ::-1, :],
-                in1=by_sin,
+                out=ra[:].rearrange("p h j (i e) -> p h j i e", e=2),
+                in0=rp[:].rearrange("p j (h i e) -> p h j i e", h=H, e=2),
+                in1=by_cos.unsqueeze(1).unsqueeze(4).to_broadcast([P, H, rows, HALF, 2]),
                 op=MULT,
             )
+            by_sin = sin[:, :, r0 : r0 + rows, :].rearrange("p e j i -> p j i e")
+            for h in range(H):
+                nc.vector.tensor_tensor(
+                    out=rb[:, h, :, :].rearrange("p j (i e) -> p j i e", e=2),
+                    in0=rp[:].rearrange("p j (h i e) -> p h j i e", h=H, e=2)[:, h, :, :, ::-1],
+                    in1=by_sin,
+                    op=MULT,
+                )
 
         def rope_add(c):
             rows = chunks[c][3]
             ra, rb = ra_t[c]
             kt = stage.tile([P, H, rows, DK], F32)
             kt_t[c] = kt
-            nc.gpsimd.tensor_tensor(
-                out=kt[:, :, :, DH:DK].rearrange("p h j (i e) -> p j h i e", e=2),
-                in0=ra[:].rearrange("p j h e i -> p j h i e"),
-                in1=rb[:].rearrange("p j h e i -> p j h i e"),
+            engine = nc.vector if c >= n - 2 else nc.gpsimd
+            engine.tensor_tensor(
+                out=kt[:, :, :, DH:DK],
+                in0=ra[:],
+                in1=rb[:],
                 op=ADD,
             )
 
@@ -292,7 +293,8 @@ def tile_multiheadlatentattention_pb_t_w8_kernel(
                     stop=True,
                 )
             dst = vt_t[c][:] if which else kt_t[c][:, :, :, 0:DH]
-            nc.scalar.copy(
+            copy = nc.vector.tensor_copy if which and c >= n - 2 else nc.scalar.copy
+            copy(
                 out=dst[:, :, 2 * half : 2 * half + 2, :].rearrange("p h j d -> p j h d"),
                 in_=acc[:].rearrange("p j (h d) -> p j h d", h=H),
             )
@@ -307,21 +309,23 @@ def tile_multiheadlatentattention_pb_t_w8_kernel(
                 )
 
         for i in range(-4, n + 1):
-            live = [k for k in range(-1, 5)]
-            on = {k: 0 <= i + k < n for k in live}
-            if on[4]:
-                widen(i + 4)
-            if i == -2:
-                order_down()
+            on = {k: 0 <= i + k < n for k in range(-1, 5)}
             if i == -1:
-                order_rope()
+                order_down()
+                order_sin()
             if on[-1]:
                 quant_d(i - 1)
+            if on[1]:
+                quant_x(i + 1)
+                if on[-1]:
+                    tick = stage.tile([P, 1], U32)
+                    nc.gpsimd.tensor_copy(out=tick[:], in_=xq_t[i + 1][0][:, 0:1])
+            if on[-1]:
                 rope_add(i - 1)
                 vt = stage.tile([P, H, chunks[i - 1][3], DH], F32)
                 vt_t[i - 1] = vt
-            if on[1]:
-                quant_x(i + 1)
+            if on[4]:
+                widen(i + 4)
             downs = []
             ups = []
             if on[0]:

@@ -21,6 +21,7 @@ DK = DH + DR
 ROWS = 4
 BLOCK = P * ROWS
 BLOCKS = S // BLOCK
+G_ROWS = 3
 
 FLOPS = 2 * B * S * D * (D + 2 * H * DH + H * DR)
 
@@ -59,7 +60,8 @@ def tile_multiheadlatentattention_pb_t_w8_kernel(
     with ExitStack() as ctx:
         keep = ctx.enter_context(tc.tile_pool(name="keep", bufs=1))
         work = ctx.enter_context(tc.tile_pool(name="work", bufs=3))
-        stage = ctx.enter_context(tc.tile_pool(name="stage", bufs=3))
+        wide = ctx.enter_context(tc.tile_pool(name="wide", bufs=9))
+        stage = ctx.enter_context(tc.tile_pool(name="stage", bufs=6))
         xt_pool = ctx.enter_context(tc.psum_pool(name="xt_pool", bufs=2))
         rope_pool = ctx.enter_context(tc.psum_pool(name="rope_pool", bufs=1))
         acc_pool = ctx.enter_context(tc.psum_pool(name="acc_pool", bufs=5))
@@ -77,12 +79,16 @@ def tile_multiheadlatentattention_pb_t_w8_kernel(
 
         x_tiles = {}
 
-        def load_x(c):
-            b, blk, row, rows = chunks[c]
-            src = x_bytes[b, blk * BLOCK : (blk + 1) * BLOCK, :].rearrange("(p j) d -> p j d", j=ROWS)
-            x_codes = keep.tile([P, rows, D], U8, name="x_codes_%d" % c)
-            nc.sync.dma_start(out=x_codes[:], in_=src[:, row : row + rows, :])
-            x_tiles[c] = x_codes
+        def load_x(b, blk, count, row, rows):
+            src = x_bytes[b, blk * BLOCK : (blk + count) * BLOCK, :].rearrange("(c p j) d -> p c j d", p=P, j=ROWS)
+            x_codes = keep.tile([P, count, rows, D], U8, name="x_codes_%d_%d_%d" % (b, blk, row))
+            nc.sync.dma_start(
+                out=x_codes[:].rearrange("p c j d -> p c (j d)"),
+                in_=src[:, :, row : row + rows, :].rearrange("p c j d -> p c (j d)"),
+            )
+            for c in range(n):
+                if chunks[c][0] == b and blk <= chunks[c][1] < blk + count and row <= chunks[c][2] < row + rows:
+                    x_tiles[c] = x_codes[:, chunks[c][1] - blk, chunks[c][2] - row : chunks[c][2] - row + chunks[c][3], :]
 
         def load_words(dst, words):
             nc.sync.dma_start(out=dst, in_=words[0].rearrange("p n t -> p (n t)").bitcast(I32))
@@ -93,35 +99,36 @@ def tile_multiheadlatentattention_pb_t_w8_kernel(
                     out=plane[r:P:32, cols].bitcast(I32), in_=scales[0, r:16:4, :].bitcast(I32)
                 )
 
-        load_x(0)
+        load_x(0, 0, 1, 0, 2)
         xs = keep.tile([P, 4], F32)
         nc.sync.dma_start(out=xs[:], in_=x_scale.rearrange("a b (p t) -> p (a b t)", t=4))
-        load_x(1)
+        load_x(0, 0, 1, 2, 2)
         down_raw = keep.tile([P, 512], I32)
         load_words(down_raw[:], down_words)
+        load_x(0, 1, 1, 0, 4)
         load_scales(down_plane, slice(0, 512), down_scales)
-        load_x(2)
+        load_x(0, 2, 2, 0, 4)
         rope_raw = keep.tile([P, P], I32, align_bytes=64)
         load_words(rope_raw[:], k_rope_words)
         load_scales(rope_plane, slice(0, P), k_rope_scales)
-        load_x(3)
-        cos = keep.tile([P, BLOCKS, ROWS, HALF], BF16)
         sin_raw = keep.tile([P, BLOCKS, ROWS, HALF], BF16)
-        nc.sync.dma_start(
-            out=cos[:].rearrange("p c j i -> p c (j i)"),
-            in_=rope_cos.rearrange("(c p j) i -> p c (j i)", p=P, j=ROWS),
-        )
         nc.sync.dma_start(
             out=sin_raw[:].rearrange("p c j i -> p c (j i)"),
             in_=rope_sin.rearrange("(c p j) i -> p c (j i)", p=P, j=ROWS),
+        )
+        cos = keep.tile([P, BLOCKS, ROWS, HALF], BF16)
+        nc.sync.dma_start(
+            out=cos[:].rearrange("p c j i -> p c (j i)"),
+            in_=rope_cos.rearrange("(c p j) i -> p c (j i)", p=P, j=ROWS),
         )
         up_codes = keep.tile([P, 512], I32, align_bytes=64)
         load_words(up_codes[:, 0:256], k_up_words)
         load_words(up_codes[:, 256:512], v_up_words)
         load_scales(up_plane, slice(0, 256), k_up_scales)
         load_scales(up_plane, slice(256, 512), v_up_scales)
-        for c in range(4, n):
-            load_x(c)
+        load_x(0, 4, 4, 0, 4)
+        load_x(1, 0, 4, 0, 4)
+        load_x(1, 4, 4, 0, 4)
 
         down_codes = keep.tile([P, 512], I32, align_bytes=64)
         down_sc = keep.tile([P, 512], U8, align_bytes=64)
@@ -144,46 +151,51 @@ def tile_multiheadlatentattention_pb_t_w8_kernel(
 
         xb_t, xt_t, gx_t, xq_t, gd_t, dq_t, rp_t, ra_t, kt_t, vt_t = {}, {}, {}, {}, {}, {}, {}, {}, {}, {}
 
+        def widen_rows(c, engine_copy, first, last):
+            xb = xb_t[c]
+            for j in range(first, last):
+                engine_copy(out=xb[:, j, :], in_=x_tiles[c][:, j, :].bitcast(FP8))
+
+        def split(c):
+            if c < 5:
+                return [0,0,2,1,1][c]
+            return chunks[c][3] * (3 if c % 2 else 3) // 4
+
         def widen(c):
-            rows = chunks[c][3]
-            xb = work.tile([P, rows, D], BF16, align_bytes=64)
+            xb = wide.tile([P, chunks[c][3], D], BF16, align_bytes=64)
             xb_t[c] = xb
-            src = x_tiles[c]
+            widen_rows(c, nc.gpsimd.tensor_copy, 0, split(c))
             if c == 0:
-                nc.scalar.copy(out=xb[:, 0, :], in_=src[:, 0, :].bitcast(FP8))
-                nc.vector.tensor_copy(out=xb[:, 1, :], in_=src[:, 1, :].bitcast(FP8))
-            elif c == 1:
-                nc.scalar.copy(out=xb[:], in_=src[:].bitcast(FP8))
-            else:
-                for j in range(rows):
-                    nc.gpsimd.tensor_copy(out=xb[:, j, :], in_=src[:, j, :].bitcast(FP8))
+                nc.scalar.copy(out=xb[:, 0, :], in_=x_tiles[c][:, 0, :].bitcast(FP8))
+                nc.vector.tensor_copy(out=xb[:, 1, :], in_=x_tiles[c][:, 1, :].bitcast(FP8))
+            if c == 1:
+                nc.scalar.copy(out=xb[:], in_=x_tiles[c].bitcast(FP8))
 
-        def transpose(c):
-            rows = chunks[c][3]
+        def widen_scalar(c):
+            if c > 1:
+                widen_rows(c, nc.scalar.copy, split(c), chunks[c][3])
+
+        def transpose(c, half):
             words = xb_t[c][:].rearrange("p j d -> p (j d)").bitcast(F32)
-            xt_t[c] = []
-            for half in range(rows // 2):
-                xt = xt_pool.tile([P, 2, 2 * P], F32)
-                xt_t[c].append(xt)
-                for jj in range(2):
-                    base = (2 * half + jj) * (D // 2)
-                    for u in range(2):
-                        nc.tensor.transpose(
-                            xt[:, u, jj * P : (jj + 1) * P], words[:, base + u : base + D // 2 : 2], ident[:]
-                        )
+            xt = xt_pool.tile([P, 2, 2 * P], F32)
+            xt_t[c, half] = xt
+            for jj in range(2):
+                base = (2 * half + jj) * (D // 2)
+                for u in range(2):
+                    nc.tensor.transpose(
+                        xt[:, u, jj * P : (jj + 1) * P], words[:, base + u : base + D // 2 : 2], ident[:]
+                    )
 
-        def scale_x(c):
-            rows = chunks[c][3]
-            gx = work.tile([P, rows * P * 4], BF16, align_bytes=64)
-            gx_t[c] = gx
-            by = xs[:].rearrange("p (u e) -> p u e", u=2).unsqueeze(1).to_broadcast([P, 2 * P, 2, 2])
-            for half in range(rows // 2):
-                nc.vector.tensor_tensor(
-                    out=gx[:, half * 1024 : (half + 1) * 1024].rearrange("p (r u e) -> p r u e", u=2, e=2),
-                    in0=xt_t[c][half][:].bitcast(BF16).rearrange("p u (r e) -> p r u e", e=2),
-                    in1=by,
-                    op=MULT,
-                )
+        def scale_x(c, half):
+            if half == 0:
+                gx = work.tile([P, chunks[c][3] * P * 4], BF16, align_bytes=64)
+                gx_t[c] = gx
+            nc.vector.tensor_tensor(
+                out=gx_t[c][:, half * 1024 : (half + 1) * 1024].rearrange("p (r u e) -> p r u e", u=2, e=2),
+                in0=xt_t[c, half][:].bitcast(BF16).rearrange("p u (r e) -> p r u e", e=2),
+                in1=xs[:].rearrange("p (u e) -> p u e", u=2).unsqueeze(1).to_broadcast([P, 2 * P, 2, 2]),
+                op=MULT,
+            )
 
         def quant_x(c):
             rows = chunks[c][3]
@@ -196,6 +208,10 @@ def tile_multiheadlatentattention_pb_t_w8_kernel(
             rows = chunks[c][3]
             gd = work.tile([P, rows * P, 4], BF16, align_bytes=64)
             gd_t[c] = gd
+            vt = stage.tile([P, H, rows, DH], F32)
+            vt_t[c] = vt
+            kt = stage.tile([P, H, rows, DK], F32)
+            kt_t[c] = kt
 
         def down(c, j):
             xc, xsc = xq_t[c]
@@ -231,13 +247,12 @@ def tile_multiheadlatentattention_pb_t_w8_kernel(
                     stop=True,
                 )
 
-        def rope_mul(c):
+        def rope_cos_mul(c):
             blk, row, rows = chunks[c][1:]
             rp = rp_t[c]
-            ra = work.tile([P, H, rows, DR], F32)
-            rb = work.tile([P, H, rows, DR], F32)
+            ra = stage.tile([P, H, rows, DR], F32)
+            rb = stage.tile([P, H, rows, DR], F32)
             ra_t[c] = (ra, rb)
-            r0 = blk * ROWS + row
             by_cos = cos[:, blk, row : row + rows, :]
             nc.vector.tensor_tensor(
                 out=ra[:].rearrange("p h j (i e) -> p h j i e", e=2),
@@ -245,6 +260,11 @@ def tile_multiheadlatentattention_pb_t_w8_kernel(
                 in1=by_cos.unsqueeze(1).unsqueeze(4).to_broadcast([P, H, rows, HALF, 2]),
                 op=MULT,
             )
+        def rope_sin_mul(c):
+            blk, row, rows = chunks[c][1:]
+            rp = rp_t[c]
+            rb = ra_t[c][1]
+            r0 = blk * ROWS + row
             by_sin = sin[:, :, r0 : r0 + rows, :].rearrange("p e j i -> p j i e")
             for h in range(H):
                 nc.vector.tensor_tensor(
@@ -255,10 +275,8 @@ def tile_multiheadlatentattention_pb_t_w8_kernel(
                 )
 
         def rope_add(c):
-            rows = chunks[c][3]
             ra, rb = ra_t[c]
-            kt = stage.tile([P, H, rows, DK], F32)
-            kt_t[c] = kt
+            kt = kt_t[c]
             engine = nc.vector if c >= n - 2 else nc.gpsimd
             engine.tensor_tensor(
                 out=kt[:, :, :, DH:DK],
@@ -308,44 +326,44 @@ def tile_multiheadlatentattention_pb_t_w8_kernel(
                     out=dst.rearrange("p h j d -> p h (j d)"), in_=tiles[c][:].rearrange("p h j d -> p h (j d)")
                 )
 
-        for i in range(-4, n + 1):
-            on = {k: 0 <= i + k < n for k in range(-1, 5)}
-            if i == -1:
-                order_down()
-                order_sin()
-            if on[-1]:
-                quant_d(i - 1)
-            if on[1]:
-                quant_x(i + 1)
-                if on[-1]:
-                    tick = stage.tile([P, 1], U32)
-                    nc.gpsimd.tensor_copy(out=tick[:], in_=xq_t[i + 1][0][:, 0:1])
-            if on[-1]:
-                rope_add(i - 1)
-                vt = stage.tile([P, H, chunks[i - 1][3], DH], F32)
-                vt_t[i - 1] = vt
-            if on[4]:
-                widen(i + 4)
-            downs = []
-            ups = []
-            if on[0]:
-                start_out(i)
-                downs = [(down, i, j) for j in range(chunks[i][3])]
-            if on[-1]:
-                ups = [(up, i - 1, which, half) for half in range(chunks[i - 1][3] // 2) for which in range(2)]
-            steps = downs[:1]
-            rest = downs[1:]
-            for k in range(max(len(rest), len(ups))):
-                steps += rest[k : k + 1] + ups[k : k + 1]
-            for k, step in enumerate(steps):
-                step[0](*step[1:])
-                if k == 1 and on[0]:
-                    rope_mm(i)
-            if on[2]:
-                scale_x(i + 2)
-            if on[0]:
-                rope_mul(i)
-            if on[3]:
-                transpose(i + 3)
-            if on[-1]:
-                store(i - 1)
+        sequence = "C00 W04 E0-1 Q01 +0-1 D00 D10 T02 T12 D20 D30 P00 S03 U0-1 U1-1 U2-1 U3-1 M02 M12 N00 A00 B00 O0-1".split()
+        for i in range(-8, n + 1):
+            for token in sequence:
+                what = token[0]
+                at = token[1]
+                c = i + int(token[2:])
+                if what == "C" and i == -1:
+                    order_down()
+                if what == "N" and i == 0:
+                    order_sin()
+                if c < 0 or c >= n:
+                    continue
+                rows = chunks[c][3]
+                if what == "W":
+                    widen(c)
+                elif what == "S":
+                    widen_scalar(c)
+                elif what == "T" and int(at) < rows // 2:
+                    transpose(c, int(at))
+                elif what == "M" and int(at) < rows // 2:
+                    scale_x(c, int(at))
+                elif what == "Q":
+                    quant_x(c)
+                elif what == "D" and int(at) < rows:
+                    if at == "0":
+                        start_out(c)
+                    down(c, int(at))
+                elif what == "P":
+                    rope_mm(c)
+                elif what == "A":
+                    rope_cos_mul(c)
+                elif what == "B":
+                    rope_sin_mul(c)
+                elif what == "+":
+                    rope_add(c)
+                elif what == "E":
+                    quant_d(c)
+                elif what == "U" and int(at) < rows:
+                    up(c, int(at) % 2, int(at) // 2)
+                elif what == "O":
+                    store(c)

from contextlib import ExitStack

import concourse.mybir as mybir
from concourse.masks import make_identity

F32 = mybir.dt.float32
BF16 = mybir.dt.bfloat16
I32 = mybir.dt.int32
U32 = mybir.dt.uint32
U8 = mybir.dt.uint8
FP8 = mybir.dt.float8_e4m3fn
FP8X4 = mybir.dt.float8_e4m3fn_x4
ADD = mybir.AluOpType.add
MULT = mybir.AluOpType.mult
COPY = mybir.ActivationFunctionType.Copy

P = 128
B, S, D, H, DH, DR = 2, 4096, 512, 2, 128, 64
HALF = DR // 2
DK = DH + DR
ROWS = 4
BLOCK = P * ROWS
BLOCKS = S // BLOCK
G_ROWS = 3

FLOPS = 2 * B * S * D * (D + 2 * H * DH + H * DR)


def tile_multiheadlatentattention_pb_t_w8_kernel(
    tc,
    x_bytes,
    x_scale,
    down_words,
    down_scales,
    k_up_words,
    k_up_scales,
    v_up_words,
    v_up_scales,
    k_rope_words,
    k_rope_scales,
    rope_cos,
    rope_sin,
    keys,
    values,
):
    nc = tc.nc

    chunks = []
    for b in range(B):
        for blk in range(BLOCKS):
            first = b == 0 and blk == 0
            last = b == B - 1 and blk == BLOCKS - 1
            if first or last:
                chunks.append((b, blk, 0, 2))
                chunks.append((b, blk, 2, 2))
            else:
                chunks.append((b, blk, 0, 4))
    n = len(chunks)

    with ExitStack() as ctx:
        keep = ctx.enter_context(tc.tile_pool(name="keep", bufs=1))
        work = ctx.enter_context(tc.tile_pool(name="work", bufs=3))
        wide = ctx.enter_context(tc.tile_pool(name="wide", bufs=9))
        stage = ctx.enter_context(tc.tile_pool(name="stage", bufs=6))
        xt_pool = ctx.enter_context(tc.psum_pool(name="xt_pool", bufs=2))
        rope_pool = ctx.enter_context(tc.psum_pool(name="rope_pool", bufs=1))
        acc_pool = ctx.enter_context(tc.psum_pool(name="acc_pool", bufs=5))
        ctx.enter_context(tc.manual_schedule())

        ident = keep.tile([P, P], F32)
        make_identity(nc, ident[:])

        down_plane = keep.tile([P, 512], U8, align_bytes=64)
        up_plane = keep.tile([P, 512], U8, align_bytes=64)
        rope_plane = keep.tile([P, P], U8, align_bytes=64)
        nc.vector.memset(down_plane[:].bitcast(I32), 0)
        nc.vector.memset(rope_plane[:].bitcast(I32), 0)
        nc.vector.memset(up_plane[:].bitcast(I32), 0)

        x_tiles = {}

        def load_x(b, blk, count, row, rows):
            src = x_bytes[b, blk * BLOCK : (blk + count) * BLOCK, :].rearrange("(c p j) d -> p c j d", p=P, j=ROWS)
            x_codes = keep.tile([P, count, rows, D], U8, name="x_codes_%d_%d_%d" % (b, blk, row))
            nc.sync.dma_start(
                out=x_codes[:].rearrange("p c j d -> p c (j d)"),
                in_=src[:, :, row : row + rows, :].rearrange("p c j d -> p c (j d)"),
            )
            for c in range(n):
                if chunks[c][0] == b and blk <= chunks[c][1] < blk + count and row <= chunks[c][2] < row + rows:
                    x_tiles[c] = x_codes[:, chunks[c][1] - blk, chunks[c][2] - row : chunks[c][2] - row + chunks[c][3], :]

        def load_words(dst, words):
            nc.sync.dma_start(out=dst, in_=words[0].rearrange("p n t -> p (n t)").bitcast(I32))

        def load_scales(plane, cols, scales):
            for r in range(4):
                nc.sync.dma_start(
                    out=plane[r:P:32, cols].bitcast(I32), in_=scales[0, r:16:4, :].bitcast(I32)
                )

        load_x(0, 0, 1, 0, 2)
        xs = keep.tile([P, 4], F32)
        nc.sync.dma_start(out=xs[:], in_=x_scale.rearrange("a b (p t) -> p (a b t)", t=4))
        load_x(0, 0, 1, 2, 2)
        down_raw = keep.tile([P, 512], I32)
        load_words(down_raw[:], down_words)
        load_x(0, 1, 1, 0, 4)
        load_scales(down_plane, slice(0, 512), down_scales)
        load_x(0, 2, 2, 0, 4)
        rope_raw = keep.tile([P, P], I32, align_bytes=64)
        load_words(rope_raw[:], k_rope_words)
        load_scales(rope_plane, slice(0, P), k_rope_scales)
        sin_raw = keep.tile([P, BLOCKS, ROWS, HALF], BF16)
        nc.sync.dma_start(
            out=sin_raw[:].rearrange("p c j i -> p c (j i)"),
            in_=rope_sin.rearrange("(c p j) i -> p c (j i)", p=P, j=ROWS),
        )
        cos = keep.tile([P, BLOCKS, ROWS, HALF], BF16)
        nc.sync.dma_start(
            out=cos[:].rearrange("p c j i -> p c (j i)"),
            in_=rope_cos.rearrange("(c p j) i -> p c (j i)", p=P, j=ROWS),
        )
        up_codes = keep.tile([P, 512], I32, align_bytes=64)
        load_words(up_codes[:, 0:256], k_up_words)
        load_words(up_codes[:, 256:512], v_up_words)
        load_scales(up_plane, slice(0, 256), k_up_scales)
        load_scales(up_plane, slice(256, 512), v_up_scales)
        load_x(0, 4, 4, 0, 4)
        load_x(1, 0, 4, 0, 4)
        load_x(1, 4, 4, 0, 4)

        down_codes = keep.tile([P, 512], I32, align_bytes=64)
        down_sc = keep.tile([P, 512], U8, align_bytes=64)
        sin = keep.tile([P, 2, BLOCKS * ROWS, HALF], BF16)

        def order_down():
            nc.vector.tensor_copy(
                out=down_codes[:].rearrange("p (t m) -> p t m", t=4),
                in_=down_raw[:].rearrange("p (m t) -> p t m", t=4),
            )
            nc.vector.tensor_copy(
                out=down_sc[:].rearrange("p (t m) -> p m t", t=4),
                in_=down_plane[:].rearrange("p (m t) -> p m t", t=4),
            )

        def order_sin():
            raw = sin_raw[:].rearrange("p c j i -> p (c j) i")
            nc.scalar.activation(out=sin[:, 0, :, :], in_=raw, func=COPY, scale=-1.0)
            nc.scalar.copy(out=sin[:, 1, :, :], in_=raw)

        xb_t, xt_t, gx_t, xq_t, gd_t, dq_t, rp_t, ra_t, kt_t, vt_t = {}, {}, {}, {}, {}, {}, {}, {}, {}, {}

        def widen_rows(c, engine_copy, first, last):
            xb = xb_t[c]
            for j in range(first, last):
                engine_copy(out=xb[:, j, :], in_=x_tiles[c][:, j, :].bitcast(FP8))

        def split(c):
            if c < 5:
                return [0,0,2,1,1][c]
            return chunks[c][3] * (3 if c % 2 else 3) // 4

        def widen(c):
            xb = wide.tile([P, chunks[c][3], D], BF16, align_bytes=64)
            xb_t[c] = xb
            widen_rows(c, nc.gpsimd.tensor_copy, 0, split(c))
            if c == 0:
                nc.scalar.copy(out=xb[:, 0, :], in_=x_tiles[c][:, 0, :].bitcast(FP8))
                nc.vector.tensor_copy(out=xb[:, 1, :], in_=x_tiles[c][:, 1, :].bitcast(FP8))
            if c == 1:
                nc.scalar.copy(out=xb[:], in_=x_tiles[c].bitcast(FP8))

        def widen_scalar(c):
            if c > 1:
                widen_rows(c, nc.scalar.copy, split(c), chunks[c][3])

        def transpose(c, half):
            words = xb_t[c][:].rearrange("p j d -> p (j d)").bitcast(F32)
            xt = xt_pool.tile([P, 2, 2 * P], F32)
            xt_t[c, half] = xt
            for jj in range(2):
                base = (2 * half + jj) * (D // 2)
                for u in range(2):
                    nc.tensor.transpose(
                        xt[:, u, jj * P : (jj + 1) * P], words[:, base + u : base + D // 2 : 2], ident[:]
                    )

        def scale_x(c, half):
            if half == 0:
                gx = work.tile([P, chunks[c][3] * P * 4], BF16, align_bytes=64)
                gx_t[c] = gx
            nc.vector.tensor_tensor(
                out=gx_t[c][:, half * 1024 : (half + 1) * 1024].rearrange("p (r u e) -> p r u e", u=2, e=2),
                in0=xt_t[c, half][:].bitcast(BF16).rearrange("p u (r e) -> p r u e", e=2),
                in1=xs[:].rearrange("p (u e) -> p u e", u=2).unsqueeze(1).to_broadcast([P, 2 * P, 2, 2]),
                op=MULT,
            )

        def quant_x(c):
            rows = chunks[c][3]
            xc = work.tile([P, rows * P], U32, align_bytes=64)
            xsc = work.tile([P, rows * P], U8, align_bytes=64)
            nc.vector.quantize_mx(out=xc[:].bitcast(FP8X4), scales=xsc[:], in_=gx_t[c][:])
            xq_t[c] = (xc, xsc)

        def start_out(c):
            rows = chunks[c][3]
            gd = work.tile([P, rows * P, 4], BF16, align_bytes=64)
            gd_t[c] = gd
            vt = stage.tile([P, H, rows, DH], F32)
            vt_t[c] = vt
            kt = stage.tile([P, H, rows, DK], F32)
            kt_t[c] = kt

        def down(c, j):
            xc, xsc = xq_t[c]
            cols = slice(j * P, (j + 1) * P)
            acc = acc_pool.tile([P, 4, P], F32)
            for t in range(4):
                w_cols = slice(t * P, (t + 1) * P)
                nc.tensor.matmul_mx(
                    out=acc[:, t, :],
                    lhsT=down_codes[:, w_cols].bitcast(FP8X4),
                    lhsT_scale=down_sc[:, w_cols],
                    rhs=xc[:, cols].bitcast(FP8X4),
                    rhs_scale=xsc[:, cols],
                    start=True,
                    stop=True,
                )
            nc.scalar.copy(out=gd_t[c][:, cols, :], in_=acc[:].rearrange("p t n -> p n t"))

        def rope_mm(c):
            xc, xsc = xq_t[c]
            rows = chunks[c][3]
            rp = rope_pool.tile([P, rows, P], F32)
            rp_t[c] = rp
            for j in range(rows):
                cols = slice(j * P, (j + 1) * P)
                nc.tensor.matmul_mx(
                    out=rp[:, j, :],
                    lhsT=xc[:, cols].bitcast(FP8X4),
                    lhsT_scale=xsc[:, cols],
                    rhs=rope_raw[:].bitcast(FP8X4),
                    rhs_scale=rope_plane[:],
                    start=True,
                    stop=True,
                )

        def rope_cos_mul(c):
            blk, row, rows = chunks[c][1:]
            rp = rp_t[c]
            ra = stage.tile([P, H, rows, DR], F32)
            rb = stage.tile([P, H, rows, DR], F32)
            ra_t[c] = (ra, rb)
            by_cos = cos[:, blk, row : row + rows, :]
            nc.vector.tensor_tensor(
                out=ra[:].rearrange("p h j (i e) -> p h j i e", e=2),
                in0=rp[:].rearrange("p j (h i e) -> p h j i e", h=H, e=2),
                in1=by_cos.unsqueeze(1).unsqueeze(4).to_broadcast([P, H, rows, HALF, 2]),
                op=MULT,
            )
        def rope_sin_mul(c):
            blk, row, rows = chunks[c][1:]
            rp = rp_t[c]
            rb = ra_t[c][1]
            r0 = blk * ROWS + row
            by_sin = sin[:, :, r0 : r0 + rows, :].rearrange("p e j i -> p j i e")
            for h in range(H):
                nc.vector.tensor_tensor(
                    out=rb[:, h, :, :].rearrange("p j (i e) -> p j i e", e=2),
                    in0=rp[:].rearrange("p j (h i e) -> p h j i e", h=H, e=2)[:, h, :, :, ::-1],
                    in1=by_sin,
                    op=MULT,
                )

        def rope_add(c):
            ra, rb = ra_t[c]
            kt = kt_t[c]
            engine = nc.vector if c >= n - 2 else nc.gpsimd
            engine.tensor_tensor(
                out=kt[:, :, :, DH:DK],
                in0=ra[:],
                in1=rb[:],
                op=ADD,
            )

        def quant_d(c):
            rows = chunks[c][3]
            dc = work.tile([P, rows * P], U32, align_bytes=64)
            dsc = work.tile([P, rows * P], U8, align_bytes=64)
            nc.vector.quantize_mx(
                out=dc[:].bitcast(FP8X4), scales=dsc[:], in_=gd_t[c][:].rearrange("p n t -> p (n t)")
            )
            dq_t[c] = (dc, dsc)

        def up(c, which, half):
            dc, dsc = dq_t[c]
            acc = acc_pool.tile([P, 2, 2 * P], F32)
            w_cols = slice(which * 256, (which + 1) * 256)
            for jj in range(2):
                j = 2 * half + jj
                cols = slice(j * P, (j + 1) * P)
                nc.tensor.matmul_mx(
                    out=acc[:, jj, :],
                    lhsT=dc[:, cols].bitcast(FP8X4),
                    lhsT_scale=dsc[:, cols],
                    rhs=up_codes[:, w_cols].bitcast(FP8X4),
                    rhs_scale=up_plane[:, w_cols],
                    start=True,
                    stop=True,
                )
            dst = vt_t[c][:] if which else kt_t[c][:, :, :, 0:DH]
            copy = nc.vector.tensor_copy if which and c >= n - 2 else nc.scalar.copy
            copy(
                out=dst[:, :, 2 * half : 2 * half + 2, :].rearrange("p h j d -> p j h d"),
                in_=acc[:].rearrange("p j (h d) -> p j h d", h=H),
            )

        def store(c):
            b, blk, row, rows = chunks[c]
            tok = slice(blk * BLOCK, (blk + 1) * BLOCK)
            for tiles, dram in ((kt_t, keys), (vt_t, values)):
                dst = dram[b, :, tok, :].rearrange("h (p j) d -> p h j d", j=ROWS)[:, :, row : row + rows, :]
                nc.sync.dma_start(
                    out=dst.rearrange("p h j d -> p h (j d)"), in_=tiles[c][:].rearrange("p h j d -> p h (j d)")
                )

        sequence = "C00 W04 E0-1 Q01 +0-1 D00 D10 T02 T12 D20 D30 P00 S03 U0-1 U1-1 U2-1 U3-1 M02 M12 N00 A00 B00 O0-1".split()
        for i in range(-8, n + 1):
            for token in sequence:
                what = token[0]
                at = token[1]
                c = i + int(token[2:])
                if what == "C" and i == -1:
                    order_down()
                if what == "N" and i == 0:
                    order_sin()
                if c < 0 or c >= n:
                    continue
                rows = chunks[c][3]
                if what == "W":
                    widen(c)
                elif what == "S":
                    widen_scalar(c)
                elif what == "T" and int(at) < rows // 2:
                    transpose(c, int(at))
                elif what == "M" and int(at) < rows // 2:
                    scale_x(c, int(at))
                elif what == "Q":
                    quant_x(c)
                elif what == "D" and int(at) < rows:
                    if at == "0":
                        start_out(c)
                    down(c, int(at))
                elif what == "P":
                    rope_mm(c)
                elif what == "A":
                    rope_cos_mul(c)
                elif what == "B":
                    rope_sin_mul(c)
                elif what == "+":
                    rope_add(c)
                elif what == "E":
                    quant_d(c)
                elif what == "U" and int(at) < rows:
                    up(c, int(at) % 2, int(at) // 2)
                elif what == "O":
                    store(c)
